import numpy as np
import ml_dtypes


def mxq(x, axis, fmt="e4m3"):
    dtype, down = {"e4m3": (ml_dtypes.float8_e4m3fn, 7), "e5m2": (ml_dtypes.float8_e5m2, 14)}[fmt]
    v = np.moveaxis(np.asarray(x, np.float32).astype(ml_dtypes.bfloat16).astype(np.float64), axis, -1)
    blocks = v.reshape(v.shape[:-1] + (-1, 32))
    amax = np.abs(blocks).max(-1, keepdims=True)
    byte = np.maximum(np.where(amax > 0, np.frexp(amax)[1] - 1 + 127, 0) - down, 1)
    scale = np.exp2(byte - 127.0)
    codes = (blocks / scale).astype(np.float32).astype(dtype).astype(np.float64)
    return np.moveaxis((codes * scale).reshape(v.shape), -1, axis)


WIDE = False


def mx_kscale(k):
    if not WIDE:
        return np.ones(k)
    levels = np.array([10, -10, 5, -5, 0])
    if k % 512:
        return np.exp2(np.random.permutation(np.resize(levels, k // 32))).repeat(32)
    a = np.empty((k // 512, 16))
    for p in range(k // 512):
        a[p, :8] = np.random.permutation(np.resize(levels, 8))
        for g in range(8):
            far = levels[np.abs(levels - a[p, g]) >= 10]
            a[p, g + 8] = far[np.random.randint(len(far))]
    return np.exp2(a.ravel()).repeat(32)


BF16 = ml_dtypes.bfloat16


def bf(x):
    return np.asarray(x, np.float32).astype(BF16)


def f64(x):
    return np.asarray(x).astype(np.float64)


E2M1 = np.array([0.0, 0.5, 1.0, 1.5, 2.0, 3.0, 4.0, 6.0, -0.0, -0.5, -1.0, -1.5, -2.0, -3.0, -4.0, -6.0])


def pack_weight(w, fmt):
    k, n = w.shape
    w = f64(bf(w)).reshape(k // 32, 32, n)
    amax = np.abs(w).max(1)
    if fmt == "e4m3":
        byte = np.frexp(amax)[1] - 1 + 127 - 7
    else:
        mant, ex = np.frexp(amax / 6.0)
        byte = np.where(mant > 0.5, ex, ex - 1) + 127
    byte = np.clip(np.where(amax > 0, byte, 1), 1, 254)
    scaled = (w * np.exp2(127.0 - byte)[:, None, :]).reshape(k, n).astype(np.float32)
    by_word = np.ascontiguousarray(scaled.reshape(k // 512, 128, 4, n).transpose(0, 1, 3, 2))
    if fmt == "e4m3":
        words = by_word.astype(ml_dtypes.float8_e4m3fn).view(np.uint8)
    else:
        c = by_word.astype(ml_dtypes.float4_e2m1fn).view(np.uint8) & 0xF
        words = c[..., 0::2] | (c[..., 1::2] << 4)
    return np.ascontiguousarray(words), np.ascontiguousarray(byte.astype(np.uint8).reshape(k // 512, 16, n))


def unpack_weight(words, scales, fmt):
    g, p, n, _ = words.shape
    if fmt == "e4m3":
        vals = np.ascontiguousarray(words).view(ml_dtypes.float8_e4m3fn).astype(np.float64)
    else:
        nib = np.empty((g, p, n, 4), np.uint8)
        nib[..., 0::2] = words & 0xF
        nib[..., 1::2] = words >> 4
        vals = E2M1[nib]
    vals = vals * np.repeat(np.exp2(scales.astype(np.float64) - 127.0), 8, axis=1)[..., None]
    return vals.transpose(0, 1, 3, 2).reshape(g * 512, n)
def pack4(w):
    words, scales = pack_weight(w, "e2m1")
    return words.reshape(words.shape[0], 128, -1), scales


def unpack4(words, scales):
    return unpack_weight(words.reshape(words.shape[0], 128, -1, 2), scales, "e2m1")


B, N, D, BD = 4, 1024, 512, 512


def draw0():
    s, u = mx_kscale(D), mx_kscale(D)
    t = mx_kscale(BD)
    keys = bf(np.random.standard_normal((B, N, D)) * s)
    values = bf(np.random.standard_normal((B, N, D)) * u)
    Wbk_words, Wbk_scales = pack4((np.random.standard_normal((BD, D)) / np.sqrt(D) / s[None, :]).T)
    bbk = bf(np.random.standard_normal(BD) * 0.1)
    Wbv_words, Wbv_scales = pack4((np.random.standard_normal((BD, D)) / np.sqrt(D) / u[None, :] * t[:, None]).T)
    bbv = bf(np.random.standard_normal(BD) * 0.1 * t)
    Wbc_words, Wbc_scales = pack4((np.random.standard_normal((D, BD)) / np.sqrt(BD) / t[None, :]).T)
    bbc = bf(np.random.standard_normal(D) * 0.1)
    return {
        "keys": keys,
        "values": values,
        "Wbk_words": Wbk_words,
        "Wbk_scales": Wbk_scales,
        "bbk": bbk,
        "Wbv_words": Wbv_words,
        "Wbv_scales": Wbv_scales,
        "bbv": bbv,
        "Wbc_words": Wbc_words,
        "Wbc_scales": Wbc_scales,
        "bbc": bbc,
    }


def core(keys, values, Wbk_words, Wbk_scales, bbk, Wbv_words, Wbv_scales, bbv, Wbc_words, Wbc_scales, bbc):
    k = (mxq(f64(keys), 2, "e4m3") @ unpack4(Wbk_words, Wbk_scales)) + f64(bbk)
    v = (mxq(f64(values), 2, "e4m3") @ unpack4(Wbv_words, Wbv_scales)) + f64(bbv)
    return (mxq(k * v, 2, "e4m3") @ unpack4(Wbc_words, Wbc_scales)) + f64(bbc)


def e4m3fn_bytes(y):
    return np.clip(np.asarray(y, np.float64), -448.0, 448.0).astype(np.float32).astype(ml_dtypes.float8_e4m3fn).view(np.uint8)


def e4m3fn_values(b):
    return np.asarray(b, np.uint8).view(ml_dtypes.float8_e4m3fn).astype(np.float64)


def setup_inputs():
    d = draw0()
    x0 = np.asarray(d['values']).astype(np.float64)
    s = (np.max(np.abs(x0), axis=(0, 1), keepdims=True) / 448.0).astype(np.float32)
    out = {}
    for k, v in d.items():
        if k == 'values':
            out['values_bytes'] = e4m3fn_bytes(x0 / s.astype(np.float64))
            out['values_scale'] = s
        else:
            out[k] = v
    return out


def reference(keys, values_bytes, values_scale, Wbk_words, Wbk_scales, bbk, Wbv_words, Wbv_scales, bbv, Wbc_words, Wbc_scales, bbc):
    return core(keys, e4m3fn_values(values_bytes) * values_scale.astype(np.float64), Wbk_words, Wbk_scales, bbk, Wbv_words, Wbv_scales, bbv, Wbc_words, Wbc_scales, bbc)

@@ -1,0 +1,240 @@
+from contextlib import ExitStack
+
+import concourse.mybir as mybir
+from concourse.masks import make_identity
+
+F32 = mybir.dt.float32
+BF16 = mybir.dt.bfloat16
+I32 = mybir.dt.int32
+U32 = mybir.dt.uint32
+U8 = mybir.dt.uint8
+E4M3 = mybir.dt.float8_e4m3fn
+E4M3X4 = mybir.dt.float8_e4m3fn_x4
+E2M1X4 = mybir.dt.float4_e2m1fn_x4
+ACT = mybir.ActivationFunctionType
+ALU = mybir.AluOpType
+
+P = 128
+PACK = 4
+D = 512
+TOKENS = 4096
+J = 2
+UNIT = P * J
+UNITS = TOKENS // UNIT
+
+FLOPS = 3 * 2 * TOKENS * D * D
+PATHS = "V"
+
+
+def tile_learnedbindingmemory_pa_t_w4_kernel(
+    tc, keys, values_bytes, values_scale, Wbk_words, Wbk_scales, bbk, Wbv_words, Wbv_scales, bbv, Wbc_words, Wbc_scales, bbc, out
+):
+    nc = tc.nc
+    keys_u = keys.rearrange("b n d -> (b n) d").rearrange("(u p j) d -> u p j d", p=P, j=J)
+    vals_u = values_bytes.rearrange("b n d -> (b n) d").rearrange("(u p j) d -> u p j d", p=P, j=J)
+    out_u = out.rearrange("b n d -> (b n) d").rearrange("(u p j) d -> u p j d", p=P, j=J)
+
+    with ExitStack() as ctx:
+        keep = ctx.enter_context(tc.tile_pool(name="keep", bufs=1))
+        loads = ctx.enter_context(tc.tile_pool(name="loads", bufs=1))
+        work = ctx.enter_context(tc.tile_pool(name="work", bufs=3))
+        psum = ctx.enter_context(tc.psum_pool(name="psum", bufs=2))
+
+        ident = keep.tile([P, P], F32)
+        make_identity(nc, ident[:])
+
+        k_in = []
+        v_in = []
+        for u in range(UNITS):
+            k_in.append(keep.tile([P, J, D], BF16, align_bytes=64, name="k_in%d" % u))
+            v_in.append(keep.tile([P, J, D], U8, align_bytes=64, name="v_in%d" % u))
+        wk_raw = keep.tile([P, PACK * P * 2], U8, align_bytes=64)
+        wv_raw = keep.tile([P, PACK * P * 2], U8, align_bytes=64)
+        wc = keep.tile([P, D * 2], U8, align_bytes=64)
+        sk_raw = keep.tile([P, D], U8, align_bytes=64)
+        sv_raw = keep.tile([P, D], U8, align_bytes=64)
+        sc = keep.tile([P, D], U8, align_bytes=64)
+        v_scale = keep.tile([P, PACK], F32)
+        bk = keep.tile([P, PACK], BF16)
+        bv = keep.tile([P, PACK], BF16)
+        bc_row = keep.tile([P, D], BF16)
+        ones = keep.tile([P, P], BF16)
+        bc = keep.tile([P, D], F32)
+        wk = keep.tile([P, PACK, P * 2], U8, align_bytes=64)
+        wv = keep.tile([P, PACK, P * 2], U8, align_bytes=64)
+        sk = keep.tile([P, PACK, P], U8, align_bytes=64)
+        sv = keep.tile([P, PACK, P], U8, align_bytes=64)
+
+        def load_values(u):
+            nc.sync.dma_start(out=v_in[u][:], in_=vals_u[u])
+
+        def load_keys(u):
+            nc.sync.dma_start(out=k_in[u][:], in_=keys_u[u])
+
+        def load_words(tile, words):
+            nc.sync.dma_start(out=tile[:].bitcast(I32), in_=words[0].bitcast(I32))
+
+        def load_scales(tile, scales):
+            for q in range(4):
+                nc.sync.dma_start(out=tile[32 * q : 32 * q + 4, :].bitcast(I32), in_=scales[0, 4 * q : 4 * q + 4, :].bitcast(I32))
+
+        def permute_words(dst, raw):
+            nc.vector.tensor_copy(out=dst[:].rearrange("p t (m b) -> p t m b", b=2), in_=raw[:].rearrange("p (m t b) -> p t m b", t=PACK, b=2))
+
+        def permute_scales(dst, raw):
+            nc.vector.tensor_copy(out=dst[:], in_=raw[:].rearrange("p (m t) -> p t m", t=PACK))
+
+        tiles = {}
+
+        def transpose_unit(u, src, name):
+            tr = psum.tile([P, 2, J, P], F32, name="tr")
+            for j in range(J):
+                words = src[:, j, :].bitcast(F32)
+                for h in range(2):
+                    nc.tensor.transpose(tr[:, h, j, :], words[:, h::2], ident[:])
+            tiles[name, u] = tr
+
+        def quantize(u, src, name):
+            codes = work.tile([P, UNIT], U32, align_bytes=64, name=name + "_codes")
+            scales = work.tile([P, UNIT], U8, align_bytes=64, name=name + "_scales")
+            nc.vector.quantize_mx(out=codes[:].bitcast(E4M3X4), scales=scales[:], in_=tiles[src, u][:].rearrange("p c t -> p (c t)"))
+            tiles[name, u] = (codes, scales)
+
+        def widen(u):
+            vb = work.tile([P, J, D], BF16, align_bytes=64, name="vb")
+            nc.scalar.copy(out=vb[:].rearrange("p j d -> p (j d)"), in_=v_in[u][:].rearrange("p j d -> p (j d)").bitcast(E4M3))
+            tiles["vb", u] = vb
+
+        def transpose_keys(u):
+            transpose_unit(u, k_in[u], "k_tr")
+
+        def transpose_values(u):
+            transpose_unit(u, tiles["vb", u], "v_tr")
+
+        def copy_keys(u):
+            kg = work.tile([P, UNIT, PACK], BF16, align_bytes=64, name="kg")
+            nc.scalar.copy(
+                out=kg[:].rearrange("p c t -> p (c t)").bitcast(F32).rearrange("p (c h) -> p c h", h=2),
+                in_=tiles["k_tr", u][:].rearrange("p h j r -> p (j r) h"),
+            )
+            tiles["kg", u] = kg
+
+        def scale_values(u):
+            vg = work.tile([P, UNIT, PACK], BF16, align_bytes=64, name="vg")
+            nc.vector.tensor_tensor(
+                out=vg[:].rearrange("p c (h e) -> p c h e", h=2),
+                in0=tiles["v_tr", u][:].rearrange("p h j r -> p (h j r)").bitcast(BF16).rearrange("p (h c e) -> p c h e", h=2, e=2),
+                in1=v_scale[:].rearrange("p (o h e) -> p o h e", o=1, h=2).to_broadcast([P, UNIT, 2, 2]),
+                op=ALU.mult,
+            )
+            tiles["vg", u] = vg
+
+        def project(u, name, weights, scales, codes):
+            data, data_scales = tiles[codes, u]
+            for h in range(2):
+                ps = psum.tile([P, 2, UNIT], F32, name=name)
+                for q in range(2):
+                    t = 2 * h + q
+                    nc.tensor.matmul_mx(
+                        out=ps[:, q, :], lhsT=weights[:, t, :].bitcast(E2M1X4), lhsT_scale=scales[:, t, :],
+                        rhs=data[:].bitcast(E4M3X4), rhs_scale=data_scales[:], start=True, stop=True,
+                    )
+                tiles[name, u, h] = ps
+
+        def project_unit(u):
+            project(u, "k_ps", wk, sk, "kc")
+            project(u, "v_ps", wv, sv, "vc")
+
+        def bias_keys(u):
+            k_sb = work.tile([P, PACK, UNIT], F32, name="k_sb")
+            tiles["k_sb", u] = k_sb
+            for t in range(PACK):
+                nc.scalar.activation(out=k_sb[:, t, :], in_=tiles["k_ps", u, t // 2][:, t % 2, :], func=ACT.Identity, bias=bk[:, t : t + 1])
+
+        def bind(u):
+            k_sb = tiles["k_sb", u]
+            planes = work.tile([P, PACK, UNIT], BF16, name="planes")
+            for t in range(PACK):
+                nc.vector.scalar_tensor_tensor(
+                    out=planes[:, t, :], in0=tiles["v_ps", u, t // 2][:, t % 2, :], scalar=bv[:, t : t + 1], in1=k_sb[:, t, :], op0=ALU.add, op1=ALU.mult
+                )
+            tiles["planes", u] = planes
+
+        def interleave(u):
+            prod = work.tile([P, UNIT, PACK], BF16, align_bytes=64, name="prod")
+            nc.scalar.copy(out=prod[:], in_=tiles["planes", u][:].rearrange("p t c -> p c t"))
+            tiles["prod", u] = prod
+
+        def combine(u):
+            codes, scales = tiles["pc", u]
+            for j in range(J):
+                o_ps = psum.tile([P, D], F32, name="o_ps")
+                cols = slice(j * P, (j + 1) * P)
+                nc.tensor.matmul_mx(
+                    out=o_ps[:], lhsT=codes[:, cols].bitcast(E4M3X4), lhsT_scale=scales[:, cols],
+                    rhs=wc[:].bitcast(E2M1X4), rhs_scale=sc[:], start=True, stop=True,
+                )
+                tiles["o_ps", u, j] = o_ps
+
+        def finish(u):
+            o_sb = work.tile([P, J, D], F32, name="o_sb")
+            for j in range(J):
+                nc.vector.tensor_tensor(out=o_sb[:, j, :], in0=tiles["o_ps", u, j][:], in1=bc[:], op=ALU.add)
+            nc.sync.dma_start(out=out_u[u], in_=o_sb[:])
+
+        def spread_bias():
+            bc_ps = psum.tile([P, D], F32, name="o_ps")
+            nc.tensor.matmul(bc_ps[:], lhsT=ones[:], rhs=bc_row[:], start=True, stop=True)
+            nc.scalar.copy(out=bc[:], in_=bc_ps[:])
+
+        with tc.manual_schedule():
+            for tile in (sk_raw, sv_raw, sc):
+                nc.vector.memset(tile[:].bitcast(I32), 0)
+            nc.vector.memset(bc_row[:], 0.0)
+            nc.vector.memset(ones[:], 1.0)
+            nc.scalar.dma_start(out=v_scale[:], in_=values_scale.rearrange("a b (p t) -> p (a b t)", t=PACK))
+            nc.scalar.dma_start(out=bk[:], in_=bbk.rearrange("(p t) -> p t", t=PACK))
+            nc.scalar.dma_start(out=bv[:], in_=bbv.rearrange("(p t) -> p t", t=PACK))
+            nc.scalar.dma_start(out=bc_row[0:1, :], in_=bbc.rearrange("(o d) -> o d", o=1))
+            load_values(0)
+            load_keys(0)
+            load_words(wk_raw, Wbk_words)
+            load_words(wv_raw, Wbv_words)
+            load_scales(sk_raw, Wbk_scales)
+            load_scales(sv_raw, Wbv_scales)
+            load_values(1)
+            load_keys(1)
+            load_values(2)
+            load_keys(2)
+            load_words(wc, Wbc_words)
+            load_scales(sc, Wbc_scales)
+            for u in range(3, UNITS):
+                load_values(u)
+                load_keys(u)
+
+            def run(fn, u):
+                if 0 <= u < UNITS:
+                    fn(u)
+
+            for i in range(-3, UNITS + 2):
+                run(bind, i)
+                run(combine, i - 1)
+                run(finish, i - 1)
+                run(copy_keys, i + 2)
+                run(transpose_values, i + 2)
+                if i == -2:
+                    permute_words(wk, wk_raw)
+                    permute_words(wv, wv_raw)
+                    spread_bias()
+                if i == -1:
+                    permute_scales(sk, sk_raw)
+                    permute_scales(sv, sv_raw)
+                run(lambda u: quantize(u, "kg", "kc"), i + 1)
+                run(lambda u: quantize(u, "vg", "vc"), i + 1)
+                run(interleave, i)
+                run(project_unit, i + 1)
+                run(widen, i + 3)
+                run(scale_values, i + 2)
+                run(lambda u: quantize(u, "prod", "pc"), i)
+                run(bias_keys, i + 1)
+                run(transpose_keys, i + 3)

@@ -23,7 +23,7 @@ UNIT = P * J
 UNITS = TOKENS // UNIT
 
 FLOPS = 3 * 2 * TOKENS * D * D
-PATHS = "V"
+VECTOR_BIAS = 1
 
 
 def tile_learnedbindingmemory_pa_t_w4_kernel(
@@ -151,19 +151,24 @@ def tile_learnedbindingmemory_pa_t_w4_kernel(
             for t in range(PACK):
                 nc.scalar.activation(out=k_sb[:, t, :], in_=tiles["k_ps", u, t // 2][:, t % 2, :], func=ACT.Identity, bias=bk[:, t : t + 1])
 
-        def bind(u):
-            k_sb = tiles["k_sb", u]
-            planes = work.tile([P, PACK, UNIT], BF16, name="planes")
+        def bias_values(u):
+            v_sb = work.tile([P, PACK, UNIT], F32, name="v_sb")
+            tiles["v_sb", u] = v_sb
             for t in range(PACK):
-                nc.vector.scalar_tensor_tensor(
-                    out=planes[:, t, :], in0=tiles["v_ps", u, t // 2][:, t % 2, :], scalar=bv[:, t : t + 1], in1=k_sb[:, t, :], op0=ALU.add, op1=ALU.mult
-                )
-            tiles["planes", u] = planes
+                src = tiles["v_ps", u, t // 2][:, t % 2, :]
+                if t < PACK - VECTOR_BIAS:
+                    nc.scalar.activation(out=v_sb[:, t, :], in_=src, func=ACT.Identity, bias=bv[:, t : t + 1])
+                else:
+                    nc.vector.tensor_scalar(out=v_sb[:, t, :], in0=src, scalar1=bv[:, t : t + 1], scalar2=None, op0=ALU.add)
 
-        def interleave(u):
+        def bind(u):
             prod = work.tile([P, UNIT, PACK], BF16, align_bytes=64, name="prod")
-            nc.scalar.copy(out=prod[:], in_=tiles["planes", u][:].rearrange("p t c -> p c t"))
             tiles["prod", u] = prod
+            for j in range(J):
+                cols = slice(j * P, (j + 1) * P)
+                nc.gpsimd.tensor_tensor(
+                    out=prod[:, cols, :], in0=tiles["v_sb", u][:, :, cols].rearrange("p t c -> p c t"), in1=tiles["k_sb", u][:, :, cols].rearrange("p t c -> p c t"), op=ALU.mult
+                )
 
         def combine(u):
             codes, scales = tiles["pc", u]
@@ -216,11 +221,11 @@ def tile_learnedbindingmemory_pa_t_w4_kernel(
                 if 0 <= u < UNITS:
                     fn(u)
 
-            for i in range(-3, UNITS + 2):
-                run(bind, i)
-                run(combine, i - 1)
-                run(finish, i - 1)
-                run(copy_keys, i + 2)
+            for i in range(-3, UNITS + 1):
+                run(bias_values, i)
+                run(lambda u: quantize(u, "kg", "kc"), i + 1)
+                run(lambda u: quantize(u, "vg", "vc"), i + 1)
+                run(lambda u: quantize(u, "prod", "pc"), i - 1)
                 run(transpose_values, i + 2)
                 if i == -2:
                     permute_words(wk, wk_raw)
@@ -229,12 +234,12 @@ def tile_learnedbindingmemory_pa_t_w4_kernel(
                 if i == -1:
                     permute_scales(sk, sk_raw)
                     permute_scales(sv, sv_raw)
-                run(lambda u: quantize(u, "kg", "kc"), i + 1)
-                run(lambda u: quantize(u, "vg", "vc"), i + 1)
-                run(interleave, i)
                 run(project_unit, i + 1)
+                run(copy_keys, i + 2)
                 run(widen, i + 3)
-                run(scale_values, i + 2)
-                run(lambda u: quantize(u, "prod", "pc"), i)
+                run(bind, i)
+                run(combine, i - 1)
                 run(bias_keys, i + 1)
+                run(scale_values, i + 2)
+                run(finish, i - 1)
                 run(transpose_keys, i + 3)

@@ -23,6 +23,7 @@ UNIT = P * J
 UNITS = TOKENS // UNIT
 
 FLOPS = 3 * 2 * TOKENS * D * D
+RUN = 4
 VECTOR_BIAS = 1
 
 
@@ -167,7 +168,10 @@ def tile_learnedbindingmemory_pa_t_w4_kernel(
             for j in range(J):
                 cols = slice(j * P, (j + 1) * P)
                 nc.gpsimd.tensor_tensor(
-                    out=prod[:, cols, :], in0=tiles["v_sb", u][:, :, cols].rearrange("p t c -> p c t"), in1=tiles["k_sb", u][:, :, cols].rearrange("p t c -> p c t"), op=ALU.mult
+                    out=prod[:, cols, :].rearrange("p (c i) t -> p c t i", i=RUN),
+                    in0=tiles["v_sb", u][:, :, cols].rearrange("p t (c i) -> p c t i", i=RUN),
+                    in1=tiles["k_sb", u][:, :, cols].rearrange("p t (c i) -> p c t i", i=RUN),
+                    op=ALU.mult,
                 )
 
         def combine(u):

@@ -18,26 +18,28 @@ P = 128
 PACK = 4
 D = 512
 TOKENS = 4096
-J = 2
-UNIT = P * J
-UNITS = TOKENS // UNIT
+J = 4
+BLOCK = P * J
+BLOCKS = TOKENS // BLOCK
+HALF = BLOCK // 2
+RUN = 4
+FIRST = 0
+SECOND = 1
+SIDES = "kv"
 
 FLOPS = 3 * 2 * TOKENS * D * D
-RUN = 4
-VECTOR_BIAS = 1
 
 
 def tile_learnedbindingmemory_pa_t_w4_kernel(
     tc, keys, values_bytes, values_scale, Wbk_words, Wbk_scales, bbk, Wbv_words, Wbv_scales, bbv, Wbc_words, Wbc_scales, bbc, out
 ):
     nc = tc.nc
-    keys_u = keys.rearrange("b n d -> (b n) d").rearrange("(u p j) d -> u p j d", p=P, j=J)
-    vals_u = values_bytes.rearrange("b n d -> (b n) d").rearrange("(u p j) d -> u p j d", p=P, j=J)
-    out_u = out.rearrange("b n d -> (b n) d").rearrange("(u p j) d -> u p j d", p=P, j=J)
+    keys_m = keys.rearrange("b n d -> (b n) d").rearrange("(m p j) d -> m p j d", p=P, j=J)
+    vals_m = values_bytes.rearrange("b n d -> (b n) d").rearrange("(m p j) d -> m p j d", p=P, j=J)
+    out_m = out.rearrange("b n d -> (b n) d").rearrange("(m p j) d -> m p j d", p=P, j=J)
 
     with ExitStack() as ctx:
         keep = ctx.enter_context(tc.tile_pool(name="keep", bufs=1))
-        loads = ctx.enter_context(tc.tile_pool(name="loads", bufs=1))
         work = ctx.enter_context(tc.tile_pool(name="work", bufs=3))
         psum = ctx.enter_context(tc.psum_pool(name="psum", bufs=2))
 
@@ -46,16 +48,18 @@ def tile_learnedbindingmemory_pa_t_w4_kernel(
 
         k_in = []
         v_in = []
-        for u in range(UNITS):
-            k_in.append(keep.tile([P, J, D], BF16, align_bytes=64, name="k_in%d" % u))
-            v_in.append(keep.tile([P, J, D], U8, align_bytes=64, name="v_in%d" % u))
+        for m in range(BLOCKS):
+            k_in.append(keep.tile([P, J, D], BF16, align_bytes=64, name="k_in%d" % m))
+            v_in.append(keep.tile([P, J, D], U8, align_bytes=64, name="v_in%d" % m))
         wk_raw = keep.tile([P, PACK * P * 2], U8, align_bytes=64)
         wv_raw = keep.tile([P, PACK * P * 2], U8, align_bytes=64)
         wc = keep.tile([P, D * 2], U8, align_bytes=64)
         sk_raw = keep.tile([P, D], U8, align_bytes=64)
         sv_raw = keep.tile([P, D], U8, align_bytes=64)
         sc = keep.tile([P, D], U8, align_bytes=64)
-        v_scale = keep.tile([P, PACK], F32)
+        v_scale = keep.tile([P, 2, D], F32)
+        scale_row = keep.tile([P, D], F32)
+        ones_f32 = keep.tile([P, P], F32)
         bk = keep.tile([P, PACK], BF16)
         bv = keep.tile([P, PACK], BF16)
         bc_row = keep.tile([P, D], BF16)
@@ -65,12 +69,6 @@ def tile_learnedbindingmemory_pa_t_w4_kernel(
         wv = keep.tile([P, PACK, P * 2], U8, align_bytes=64)
         sk = keep.tile([P, PACK, P], U8, align_bytes=64)
         sv = keep.tile([P, PACK, P], U8, align_bytes=64)
-
-        def load_values(u):
-            nc.sync.dma_start(out=v_in[u][:], in_=vals_u[u])
-
-        def load_keys(u):
-            nc.sync.dma_start(out=k_in[u][:], in_=keys_u[u])
 
         def load_words(tile, words):
             nc.sync.dma_start(out=tile[:].bitcast(I32), in_=words[0].bitcast(I32))
@@ -87,163 +85,237 @@ def tile_learnedbindingmemory_pa_t_w4_kernel(
 
         tiles = {}
 
-        def transpose_unit(u, src, name):
-            tr = psum.tile([P, 2, J, P], F32, name="tr")
-            for j in range(J):
-                words = src[:, j, :].bitcast(F32)
-                for h in range(2):
-                    nc.tensor.transpose(tr[:, h, j, :], words[:, h::2], ident[:])
-            tiles[name, u] = tr
+        def half_cols(h):
+            return slice(h * HALF, (h + 1) * HALF)
 
-        def quantize(u, src, name):
-            codes = work.tile([P, UNIT], U32, align_bytes=64, name=name + "_codes")
-            scales = work.tile([P, UNIT], U8, align_bytes=64, name=name + "_scales")
-            nc.vector.quantize_mx(out=codes[:].bitcast(E4M3X4), scales=scales[:], in_=tiles[src, u][:].rearrange("p c t -> p (c t)"))
-            tiles[name, u] = (codes, scales)
-
-        def widen(u):
-            vb = work.tile([P, J, D], BF16, align_bytes=64, name="vb")
-            nc.scalar.copy(out=vb[:].rearrange("p j d -> p (j d)"), in_=v_in[u][:].rearrange("p j d -> p (j d)").bitcast(E4M3))
-            tiles["vb", u] = vb
-
-        def transpose_keys(u):
-            transpose_unit(u, k_in[u], "k_tr")
-
-        def transpose_values(u):
-            transpose_unit(u, tiles["vb", u], "v_tr")
-
-        def copy_keys(u):
-            kg = work.tile([P, UNIT, PACK], BF16, align_bytes=64, name="kg")
-            nc.scalar.copy(
-                out=kg[:].rearrange("p c t -> p (c t)").bitcast(F32).rearrange("p (c h) -> p c h", h=2),
-                in_=tiles["k_tr", u][:].rearrange("p h j r -> p (j r) h"),
-            )
-            tiles["kg", u] = kg
-
-        def scale_values(u):
-            vg = work.tile([P, UNIT, PACK], BF16, align_bytes=64, name="vg")
+        def scale_values(m, h):
+            tiles["scaled", m, h] = work.tile([P, 2, D], BF16, align_bytes=64, name="scaled")
             nc.vector.tensor_tensor(
-                out=vg[:].rearrange("p c (h e) -> p c h e", h=2),
-                in0=tiles["v_tr", u][:].rearrange("p h j r -> p (h j r)").bitcast(BF16).rearrange("p (h c e) -> p c h e", h=2, e=2),
-                in1=v_scale[:].rearrange("p (o h e) -> p o h e", o=1, h=2).to_broadcast([P, UNIT, 2, 2]),
+                out=tiles["scaled", m, h][:].rearrange("p j d -> p (j d)"),
+                in0=v_in[m][:, 2 * h : 2 * h + 2, :].rearrange("p j d -> p (j d)").bitcast(E4M3),
+                in1=v_scale[:].rearrange("p j d -> p (j d)"),
                 op=ALU.mult,
             )
-            tiles["vg", u] = vg
 
-        def project(u, name, weights, scales, codes):
-            data, data_scales = tiles[codes, u]
-            for h in range(2):
-                ps = psum.tile([P, 2, UNIT], F32, name=name)
+        def transpose(m, h, side):
+            src = k_in[m][:, 2 * h : 2 * h + 2, :] if side == "k" else tiles["scaled", m, h]
+            tr = psum.tile([P, 2, 2, P], F32, name="tr")
+            for j in range(2):
+                words = src[:, j, :].bitcast(F32)
+                for e in range(2):
+                    nc.tensor.transpose(tr[:, e, j, :], words[:, e::2], ident[:])
+            tiles[side + "_tr", m, h] = tr
+
+        def copy_out(m, h, side):
+            if side == "k":
+                tiles["grouped", m, h] = work.tile([P, 2, HALF, PACK], BF16, align_bytes=64, name="grouped")
+            grouped = tiles["grouped", m, h][:, SIDES.index(side), :, :]
+            nc.scalar.copy(
+                out=grouped.rearrange("p c t -> p (c t)").bitcast(F32).rearrange("p (c e) -> p c e", e=2),
+                in_=tiles[side + "_tr", m, h][:].rearrange("p e j r -> p (j r) e"),
+            )
+
+        def quantize(codes, scales, grouped):
+            nc.vector.quantize_mx(out=codes.bitcast(E4M3X4), scales=scales, in_=grouped)
+
+        def quantize_inputs(m, h, sides=SIDES):
+            if sides[0] == "k":
+                codes = work.tile([P, 2 * HALF], U32, align_bytes=64, name="kv_codes")
+                scales = work.tile([P, 2 * HALF], U8, align_bytes=64, name="kv_scales")
+                tiles["kv", m, h] = (codes, scales)
+            codes, scales = tiles["kv", m, h]
+            s0, s1 = SIDES.index(sides[0]), SIDES.index(sides[-1]) + 1
+            cols = slice(s0 * HALF, s1 * HALF)
+            quantize(codes[:, cols], scales[:, cols], tiles["grouped", m, h][:, s0:s1, :, :].rearrange("p s c t -> p (s c t)"))
+
+        def quantize_product(m, h):
+            last = m == BLOCKS - 1
+            if h == FIRST and not last:
+                return
+            if ("p", m) not in tiles:
+                codes = work.tile([P, BLOCK], U32, align_bytes=64, name="p_codes")
+                scales = work.tile([P, BLOCK], U8, align_bytes=64, name="p_scales")
+                tiles["p", m] = (codes, scales)
+            codes, scales = tiles["p", m]
+            cols = half_cols(h) if last else slice(0, BLOCK)
+            quantize(codes[:, cols], scales[:, cols], product(m)[:, cols, :].rearrange("p c t -> p (c t)"))
+
+        def project(m, h, side):
+            weights, w_scales = (wk, sk) if side == "k" else (wv, sv)
+            codes, scales = tiles["kv", m, h]
+            cols = slice(SIDES.index(side) * HALF, (SIDES.index(side) + 1) * HALF)
+            for g in range(2):
+                ps = psum.tile([P, 2, HALF], F32, name=side + "_ps")
                 for q in range(2):
-                    t = 2 * h + q
+                    t = 2 * g + q
                     nc.tensor.matmul_mx(
-                        out=ps[:, q, :], lhsT=weights[:, t, :].bitcast(E2M1X4), lhsT_scale=scales[:, t, :],
-                        rhs=data[:].bitcast(E4M3X4), rhs_scale=data_scales[:], start=True, stop=True,
+                        out=ps[:, q, :], lhsT=weights[:, t, :].bitcast(E2M1X4), lhsT_scale=w_scales[:, t, :],
+                        rhs=codes[:, cols].bitcast(E4M3X4), rhs_scale=scales[:, cols], start=True, stop=True,
                     )
-                tiles[name, u, h] = ps
+                tiles[side + "_ps", m, h, g] = ps
 
-        def project_unit(u):
-            project(u, "k_ps", wk, sk, "kc")
-            project(u, "v_ps", wv, sv, "vc")
-
-        def bias_keys(u):
-            k_sb = work.tile([P, PACK, UNIT], F32, name="k_sb")
-            tiles["k_sb", u] = k_sb
+        def add_bias(m, h, side):
+            sb = work.tile([P, PACK, HALF], F32, name=side + "_sb")
+            bias = bk if side == "k" else bv
             for t in range(PACK):
-                nc.scalar.activation(out=k_sb[:, t, :], in_=tiles["k_ps", u, t // 2][:, t % 2, :], func=ACT.Identity, bias=bk[:, t : t + 1])
+                nc.scalar.activation(out=sb[:, t, :], in_=tiles[side + "_ps", m, h, t // 2][:, t % 2, :], func=ACT.Identity, bias=bias[:, t : t + 1])
+            tiles[side + "_sb", m, h] = sb
 
-        def bias_values(u):
-            v_sb = work.tile([P, PACK, UNIT], F32, name="v_sb")
-            tiles["v_sb", u] = v_sb
-            for t in range(PACK):
-                src = tiles["v_ps", u, t // 2][:, t % 2, :]
-                if t < PACK - VECTOR_BIAS:
-                    nc.scalar.activation(out=v_sb[:, t, :], in_=src, func=ACT.Identity, bias=bv[:, t : t + 1])
-                else:
-                    nc.vector.tensor_scalar(out=v_sb[:, t, :], in0=src, scalar1=bv[:, t : t + 1], scalar2=None, op0=ALU.add)
+        def product(m):
+            if ("p_grouped", m) not in tiles:
+                tiles["p_grouped", m] = work.tile([P, BLOCK, PACK], BF16, align_bytes=64, name="p_grouped")
+            return tiles["p_grouped", m]
 
-        def bind(u):
-            prod = work.tile([P, UNIT, PACK], BF16, align_bytes=64, name="prod")
-            tiles["prod", u] = prod
-            for j in range(J):
+        def bind_on_gpsimd(m):
+            nc.vector.memset(product(m)[:, 0, :], 0.0)
+            for j in range(2):
                 cols = slice(j * P, (j + 1) * P)
                 nc.gpsimd.tensor_tensor(
-                    out=prod[:, cols, :].rearrange("p (c i) t -> p c t i", i=RUN),
-                    in0=tiles["v_sb", u][:, :, cols].rearrange("p t (c i) -> p c t i", i=RUN),
-                    in1=tiles["k_sb", u][:, :, cols].rearrange("p t (c i) -> p c t i", i=RUN),
+                    out=product(m)[:, cols, :].rearrange("p (c i) t -> p c t i", i=RUN),
+                    in0=tiles["v_sb", m, FIRST][:, :, cols].rearrange("p t (c i) -> p c t i", i=RUN),
+                    in1=tiles["k_sb", m, FIRST][:, :, cols].rearrange("p t (c i) -> p c t i", i=RUN),
                     op=ALU.mult,
                 )
 
-        def combine(u):
-            codes, scales = tiles["pc", u]
-            for j in range(J):
-                o_ps = psum.tile([P, D], F32, name="o_ps")
-                cols = slice(j * P, (j + 1) * P)
-                nc.tensor.matmul_mx(
-                    out=o_ps[:], lhsT=codes[:, cols].bitcast(E4M3X4), lhsT_scale=scales[:, cols],
-                    rhs=wc[:].bitcast(E2M1X4), rhs_scale=sc[:], start=True, stop=True,
+        def bind_on_vector(m, h):
+            planes = work.tile([P, PACK, HALF], BF16, name="planes")
+            for t in range(PACK):
+                nc.vector.scalar_tensor_tensor(
+                    out=planes[:, t, :], in0=tiles["v_ps", m, h, t // 2][:, t % 2, :], scalar=bv[:, t : t + 1],
+                    in1=tiles["k_sb", m, h][:, t, :], op0=ALU.add, op1=ALU.mult,
                 )
-                tiles["o_ps", u, j] = o_ps
+            tiles["planes", m, h] = planes
 
-        def finish(u):
-            o_sb = work.tile([P, J, D], F32, name="o_sb")
-            for j in range(J):
-                nc.vector.tensor_tensor(out=o_sb[:, j, :], in0=tiles["o_ps", u, j][:], in1=bc[:], op=ALU.add)
-            nc.sync.dma_start(out=out_u[u], in_=o_sb[:])
+        def interleave(m, h):
+            dst = product(m)[:, half_cols(h), :]
+            src = tiles["planes", m, h][:].rearrange("p t c -> p c t")
+            if m == BLOCKS - 1:
+                nc.vector.tensor_copy(out=dst, in_=src)
+            else:
+                nc.scalar.copy(out=dst, in_=src)
+
+        def combine(m, j):
+            codes, scales = tiles["p", m]
+            cols = slice(j * P, (j + 1) * P)
+            o_ps = psum.tile([P, D], F32, name="o_ps")
+            nc.tensor.matmul_mx(
+                out=o_ps[:], lhsT=codes[:, cols].bitcast(E4M3X4), lhsT_scale=scales[:, cols],
+                rhs=wc[:].bitcast(E2M1X4), rhs_scale=sc[:], start=True, stop=True,
+            )
+            tiles["o_ps", m, j] = o_ps
+
+        def finish(m, j):
+            if j % 2 == 0:
+                tiles["o_sb", m] = work.tile([P, 2, D], F32, name="o_sb")
+            o_sb = tiles["o_sb", m]
+            nc.vector.tensor_tensor(out=o_sb[:, j % 2, :], in0=tiles["o_ps", m, j][:], in1=bc[:], op=ALU.add)
+            if m == BLOCKS - 1:
+                nc.sync.dma_start(out=out_m[m, :, j, :], in_=o_sb[:, j % 2, :])
+            elif j % 2 == 1:
+                nc.sync.dma_start(out=out_m[m, :, j - 1 : j + 1, :], in_=o_sb[:])
 
         def spread_bias():
             bc_ps = psum.tile([P, D], F32, name="o_ps")
             nc.tensor.matmul(bc_ps[:], lhsT=ones[:], rhs=bc_row[:], start=True, stop=True)
             nc.scalar.copy(out=bc[:], in_=bc_ps[:])
 
+        def spread_scale():
+            tiles["scale"] = psum.tile([P, D], F32, name="o_ps")
+            nc.tensor.matmul(tiles["scale"][:], lhsT=ones_f32[:], rhs=scale_row[:], start=True, stop=True)
+
+        def copy_scale():
+            for j in range(2):
+                nc.scalar.copy(out=v_scale[:, j, :], in_=tiles["scale"][:])
+
+        issued = set()
+
+        def once(call, m, *args):
+            if 0 <= m < BLOCKS and (call, m, args) not in issued:
+                issued.add((call, m, args))
+                call(m, *args)
+
         with tc.manual_schedule():
-            for tile in (sk_raw, sv_raw, sc):
-                nc.vector.memset(tile[:].bitcast(I32), 0)
+            nc.vector.memset(scale_row[:], 0.0)
+            nc.vector.memset(sk_raw[:].bitcast(I32), 0)
+            nc.vector.memset(ones_f32[:], 1.0)
+            nc.vector.memset(sv_raw[:].bitcast(I32), 0)
             nc.vector.memset(bc_row[:], 0.0)
+            nc.vector.memset(sc[:].bitcast(I32), 0)
             nc.vector.memset(ones[:], 1.0)
-            nc.scalar.dma_start(out=v_scale[:], in_=values_scale.rearrange("a b (p t) -> p (a b t)", t=PACK))
-            nc.scalar.dma_start(out=bk[:], in_=bbk.rearrange("(p t) -> p t", t=PACK))
-            nc.scalar.dma_start(out=bv[:], in_=bbv.rearrange("(p t) -> p t", t=PACK))
-            nc.scalar.dma_start(out=bc_row[0:1, :], in_=bbc.rearrange("(o d) -> o d", o=1))
-            load_values(0)
-            load_keys(0)
+            nc.scalar.dma_start(out=scale_row[0:1, :], in_=values_scale[0])
+            nc.sync.dma_start(out=k_in[0][:, 0:2, :], in_=keys_m[0, :, 0:2, :])
             load_words(wk_raw, Wbk_words)
-            load_words(wv_raw, Wbv_words)
+            nc.sync.dma_start(out=v_in[0][:], in_=vals_m[0])
             load_scales(sk_raw, Wbk_scales)
+            nc.gpsimd.dma_start(out=k_in[0][:, 2:4, :], in_=keys_m[0, :, 2:4, :])
+            nc.gpsimd.dma_start(out=bk[:], in_=bbk.rearrange("(p t) -> p t", t=PACK))
+            nc.gpsimd.dma_start(out=bv[:], in_=bbv.rearrange("(p t) -> p t", t=PACK))
+            nc.gpsimd.dma_start(out=bc_row[0:1, :], in_=bbc.rearrange("(o d) -> o d", o=1))
+            load_words(wv_raw, Wbv_words)
             load_scales(sv_raw, Wbv_scales)
-            load_values(1)
-            load_keys(1)
-            load_values(2)
-            load_keys(2)
+            nc.sync.dma_start(out=v_in[1][:], in_=vals_m[1])
+            nc.sync.dma_start(out=k_in[1][:], in_=keys_m[1])
             load_words(wc, Wbc_words)
             load_scales(sc, Wbc_scales)
-            for u in range(3, UNITS):
-                load_values(u)
-                load_keys(u)
+            for m in range(2, BLOCKS):
+                nc.sync.dma_start(out=v_in[m][:], in_=vals_m[m])
+                nc.sync.dma_start(out=k_in[m][:], in_=keys_m[m])
 
-            def run(fn, u):
-                if 0 <= u < UNITS:
-                    fn(u)
-
-            for i in range(-3, UNITS + 1):
-                run(bias_values, i)
-                run(lambda u: quantize(u, "kg", "kc"), i + 1)
-                run(lambda u: quantize(u, "vg", "vc"), i + 1)
-                run(lambda u: quantize(u, "prod", "pc"), i - 1)
-                run(transpose_values, i + 2)
-                if i == -2:
-                    permute_words(wk, wk_raw)
-                    permute_words(wv, wv_raw)
-                    spread_bias()
-                if i == -1:
-                    permute_scales(sk, sk_raw)
-                    permute_scales(sv, sv_raw)
-                run(project_unit, i + 1)
-                run(copy_keys, i + 2)
-                run(widen, i + 3)
-                run(bind, i)
-                run(combine, i - 1)
-                run(bias_keys, i + 1)
-                run(scale_values, i + 2)
-                run(finish, i - 1)
-                run(transpose_keys, i + 3)
+            spread_scale()
+            permute_words(wk, wk_raw)
+            permute_scales(sk, sk_raw)
+            permute_words(wv, wv_raw)
+            copy_scale()
+            once(transpose, 0, FIRST, "k")
+            once(copy_out, 0, FIRST, "k")
+            once(transpose, 0, SECOND, "k")
+            once(copy_out, 0, SECOND, "k")
+            once(scale_values, 0, FIRST)
+            once(transpose, 0, FIRST, "v")
+            once(scale_values, 0, SECOND)
+            permute_scales(sv, sv_raw)
+            once(copy_out, 0, FIRST, "v")
+            once(transpose, 0, SECOND, "v")
+            once(copy_out, 0, SECOND, "v")
+            once(quantize_inputs, 0, FIRST)
+            once(project, 0, FIRST, "k")
+            once(scale_values, 1, FIRST)
+            once(project, 0, FIRST, "v")
+            once(add_bias, 0, FIRST, "k")
+            once(add_bias, 0, FIRST, "v")
+            once(transpose, 1, FIRST, "k")
+            once(transpose, 1, FIRST, "v")
+            spread_bias()
+            for m in range(BLOCKS + 2):
+                once(quantize_product, m - 1, SECOND)
+                once(copy_out, m, SECOND, "v")
+                once(quantize_inputs, m, SECOND)
+                once(add_bias, m, FIRST, "k")
+                once(project, m, FIRST, "v")
+                once(add_bias, m, FIRST, "v")
+                once(copy_out, m + 1, FIRST, "k")
+                once(project, m, SECOND, "k")
+                once(scale_values, m + 1, SECOND)
+                once(combine, m - 1, 0)
+                once(bind_on_gpsimd, m)
+                once(combine, m - 1, 1)
+                once(project, m, SECOND, "v")
+                once(add_bias, m, SECOND, "k")
+                once(finish, m - 1, 0)
+                once(transpose, m + 1, FIRST, "v")
+                once(copy_out, m + 1, FIRST, "v")
+                once(transpose, m + 1, SECOND, "k")
+                once(combine, m - 1, 2)
+                once(finish, m - 1, 1)
+                once(combine, m - 1, 3)
+                once(bind_on_vector, m, SECOND)
+                once(transpose, m + 1, SECOND, "v")
+                once(copy_out, m + 1, SECOND, "k")
+                once(finish, m - 1, 2)
+                once(finish, m - 1, 3)
+                once(quantize_product, m, FIRST)
+                once(quantize_inputs, m + 1, FIRST)
+                once(scale_values, m + 2, FIRST)
+                once(transpose, m + 2, FIRST, "k")
+                once(project, m + 1, FIRST, "k")
+                once(interleave, m, SECOND)

from contextlib import ExitStack

import concourse.mybir as mybir
from concourse.masks import make_identity

F32 = mybir.dt.float32
BF16 = mybir.dt.bfloat16
I32 = mybir.dt.int32
U32 = mybir.dt.uint32
U8 = mybir.dt.uint8
E4M3 = mybir.dt.float8_e4m3fn
E4M3X4 = mybir.dt.float8_e4m3fn_x4
E2M1X4 = mybir.dt.float4_e2m1fn_x4
ACT = mybir.ActivationFunctionType
ALU = mybir.AluOpType

P = 128
PACK = 4
D = 512
TOKENS = 4096
J = 4
BLOCK = P * J
BLOCKS = TOKENS // BLOCK
HALF = BLOCK // 2
RUN = 4
FIRST = 0
SECOND = 1
SIDES = "kv"

FLOPS = 3 * 2 * TOKENS * D * D


def tile_learnedbindingmemory_pa_t_w4_kernel(
    tc, keys, values_bytes, values_scale, Wbk_words, Wbk_scales, bbk, Wbv_words, Wbv_scales, bbv, Wbc_words, Wbc_scales, bbc, out
):
    nc = tc.nc
    keys_m = keys.rearrange("b n d -> (b n) d").rearrange("(m p j) d -> m p j d", p=P, j=J)
    vals_m = values_bytes.rearrange("b n d -> (b n) d").rearrange("(m p j) d -> m p j d", p=P, j=J)
    out_m = out.rearrange("b n d -> (b n) d").rearrange("(m p j) d -> m p j d", p=P, j=J)

    with ExitStack() as ctx:
        keep = ctx.enter_context(tc.tile_pool(name="keep", bufs=1))
        work = ctx.enter_context(tc.tile_pool(name="work", bufs=3))
        psum = ctx.enter_context(tc.psum_pool(name="psum", bufs=2))

        ident = keep.tile([P, P], F32)
        make_identity(nc, ident[:])

        k_in = []
        v_in = []
        for m in range(BLOCKS):
            k_in.append(keep.tile([P, J, D], BF16, align_bytes=64, name="k_in%d" % m))
            v_in.append(keep.tile([P, J, D], U8, align_bytes=64, name="v_in%d" % m))
        wk_raw = keep.tile([P, PACK * P * 2], U8, align_bytes=64)
        wv_raw = keep.tile([P, PACK * P * 2], U8, align_bytes=64)
        wc = keep.tile([P, D * 2], U8, align_bytes=64)
        sk_raw = keep.tile([P, D], U8, align_bytes=64)
        sv_raw = keep.tile([P, D], U8, align_bytes=64)
        sc = keep.tile([P, D], U8, align_bytes=64)
        v_scale = keep.tile([P, 2, D], F32)
        scale_row = keep.tile([P, D], F32)
        ones_f32 = keep.tile([P, P], F32)
        bk = keep.tile([P, PACK], BF16)
        bv = keep.tile([P, PACK], BF16)
        bc_row = keep.tile([P, D], BF16)
        ones = keep.tile([P, P], BF16)
        bc = keep.tile([P, D], F32)
        wk = keep.tile([P, PACK, P * 2], U8, align_bytes=64)
        wv = keep.tile([P, PACK, P * 2], U8, align_bytes=64)
        sk = keep.tile([P, PACK, P], U8, align_bytes=64)
        sv = keep.tile([P, PACK, P], U8, align_bytes=64)

        def load_words(tile, words):
            nc.sync.dma_start(out=tile[:].bitcast(I32), in_=words[0].bitcast(I32))

        def load_scales(tile, scales):
            for q in range(4):
                nc.sync.dma_start(out=tile[32 * q : 32 * q + 4, :].bitcast(I32), in_=scales[0, 4 * q : 4 * q + 4, :].bitcast(I32))

        def permute_words(dst, raw):
            nc.vector.tensor_copy(out=dst[:].rearrange("p t (m b) -> p t m b", b=2), in_=raw[:].rearrange("p (m t b) -> p t m b", t=PACK, b=2))

        def permute_scales(dst, raw):
            nc.vector.tensor_copy(out=dst[:], in_=raw[:].rearrange("p (m t) -> p t m", t=PACK))

        tiles = {}

        def half_cols(h):
            return slice(h * HALF, (h + 1) * HALF)

        def scale_values(m, h):
            tiles["scaled", m, h] = work.tile([P, 2, D], BF16, align_bytes=64, name="scaled")
            nc.vector.tensor_tensor(
                out=tiles["scaled", m, h][:].rearrange("p j d -> p (j d)"),
                in0=v_in[m][:, 2 * h : 2 * h + 2, :].rearrange("p j d -> p (j d)").bitcast(E4M3),
                in1=v_scale[:].rearrange("p j d -> p (j d)"),
                op=ALU.mult,
            )

        def transpose(m, h, side):
            src = k_in[m][:, 2 * h : 2 * h + 2, :] if side == "k" else tiles["scaled", m, h]
            tr = psum.tile([P, 2, 2, P], F32, name="tr")
            for j in range(2):
                words = src[:, j, :].bitcast(F32)
                for e in range(2):
                    nc.tensor.transpose(tr[:, e, j, :], words[:, e::2], ident[:])
            tiles[side + "_tr", m, h] = tr

        def copy_out(m, h, side):
            if side == "k":
                tiles["grouped", m, h] = work.tile([P, 2, HALF, PACK], BF16, align_bytes=64, name="grouped")
            grouped = tiles["grouped", m, h][:, SIDES.index(side), :, :]
            nc.scalar.copy(
                out=grouped.rearrange("p c t -> p (c t)").bitcast(F32).rearrange("p (c e) -> p c e", e=2),
                in_=tiles[side + "_tr", m, h][:].rearrange("p e j r -> p (j r) e"),
            )

        def quantize(codes, scales, grouped):
            nc.vector.quantize_mx(out=codes.bitcast(E4M3X4), scales=scales, in_=grouped)

        def quantize_inputs(m, h, sides=SIDES):
            if sides[0] == "k":
                codes = work.tile([P, 2 * HALF], U32, align_bytes=64, name="kv_codes")
                scales = work.tile([P, 2 * HALF], U8, align_bytes=64, name="kv_scales")
                tiles["kv", m, h] = (codes, scales)
            codes, scales = tiles["kv", m, h]
            s0, s1 = SIDES.index(sides[0]), SIDES.index(sides[-1]) + 1
            cols = slice(s0 * HALF, s1 * HALF)
            quantize(codes[:, cols], scales[:, cols], tiles["grouped", m, h][:, s0:s1, :, :].rearrange("p s c t -> p (s c t)"))

        def quantize_product(m, h):
            last = m == BLOCKS - 1
            if h == FIRST and not last:
                return
            if ("p", m) not in tiles:
                codes = work.tile([P, BLOCK], U32, align_bytes=64, name="p_codes")
                scales = work.tile([P, BLOCK], U8, align_bytes=64, name="p_scales")
                tiles["p", m] = (codes, scales)
            codes, scales = tiles["p", m]
            cols = half_cols(h) if last else slice(0, BLOCK)
            quantize(codes[:, cols], scales[:, cols], product(m)[:, cols, :].rearrange("p c t -> p (c t)"))

        def project(m, h, side):
            weights, w_scales = (wk, sk) if side == "k" else (wv, sv)
            codes, scales = tiles["kv", m, h]
            cols = slice(SIDES.index(side) * HALF, (SIDES.index(side) + 1) * HALF)
            for g in range(2):
                ps = psum.tile([P, 2, HALF], F32, name=side + "_ps")
                for q in range(2):
                    t = 2 * g + q
                    nc.tensor.matmul_mx(
                        out=ps[:, q, :], lhsT=weights[:, t, :].bitcast(E2M1X4), lhsT_scale=w_scales[:, t, :],
                        rhs=codes[:, cols].bitcast(E4M3X4), rhs_scale=scales[:, cols], start=True, stop=True,
                    )
                tiles[side + "_ps", m, h, g] = ps

        def add_bias(m, h, side):
            sb = work.tile([P, PACK, HALF], F32, name=side + "_sb")
            bias = bk if side == "k" else bv
            for t in range(PACK):
                nc.scalar.activation(out=sb[:, t, :], in_=tiles[side + "_ps", m, h, t // 2][:, t % 2, :], func=ACT.Identity, bias=bias[:, t : t + 1])
            tiles[side + "_sb", m, h] = sb

        def product(m):
            if ("p_grouped", m) not in tiles:
                tiles["p_grouped", m] = work.tile([P, BLOCK, PACK], BF16, align_bytes=64, name="p_grouped")
            return tiles["p_grouped", m]

        def bind_on_gpsimd(m):
            nc.vector.memset(product(m)[:, 0, :], 0.0)
            for j in range(2):
                cols = slice(j * P, (j + 1) * P)
                nc.gpsimd.tensor_tensor(
                    out=product(m)[:, cols, :].rearrange("p (c i) t -> p c t i", i=RUN),
                    in0=tiles["v_sb", m, FIRST][:, :, cols].rearrange("p t (c i) -> p c t i", i=RUN),
                    in1=tiles["k_sb", m, FIRST][:, :, cols].rearrange("p t (c i) -> p c t i", i=RUN),
                    op=ALU.mult,
                )

        def bind_on_vector(m, h):
            planes = work.tile([P, PACK, HALF], BF16, name="planes")
            for t in range(PACK):
                nc.vector.scalar_tensor_tensor(
                    out=planes[:, t, :], in0=tiles["v_ps", m, h, t // 2][:, t % 2, :], scalar=bv[:, t : t + 1],
                    in1=tiles["k_sb", m, h][:, t, :], op0=ALU.add, op1=ALU.mult,
                )
            tiles["planes", m, h] = planes

        def interleave(m, h):
            dst = product(m)[:, half_cols(h), :]
            src = tiles["planes", m, h][:].rearrange("p t c -> p c t")
            if m == BLOCKS - 1:
                nc.vector.tensor_copy(out=dst, in_=src)
            else:
                nc.scalar.copy(out=dst, in_=src)

        def combine(m, j):
            codes, scales = tiles["p", m]
            cols = slice(j * P, (j + 1) * P)
            o_ps = psum.tile([P, D], F32, name="o_ps")
            nc.tensor.matmul_mx(
                out=o_ps[:], lhsT=codes[:, cols].bitcast(E4M3X4), lhsT_scale=scales[:, cols],
                rhs=wc[:].bitcast(E2M1X4), rhs_scale=sc[:], start=True, stop=True,
            )
            tiles["o_ps", m, j] = o_ps

        def finish(m, j):
            if j % 2 == 0:
                tiles["o_sb", m] = work.tile([P, 2, D], F32, name="o_sb")
            o_sb = tiles["o_sb", m]
            nc.vector.tensor_tensor(out=o_sb[:, j % 2, :], in0=tiles["o_ps", m, j][:], in1=bc[:], op=ALU.add)
            if m == BLOCKS - 1:
                nc.sync.dma_start(out=out_m[m, :, j, :], in_=o_sb[:, j % 2, :])
            elif j % 2 == 1:
                nc.sync.dma_start(out=out_m[m, :, j - 1 : j + 1, :], in_=o_sb[:])

        def spread_bias():
            bc_ps = psum.tile([P, D], F32, name="o_ps")
            nc.tensor.matmul(bc_ps[:], lhsT=ones[:], rhs=bc_row[:], start=True, stop=True)
            nc.scalar.copy(out=bc[:], in_=bc_ps[:])

        def spread_scale():
            tiles["scale"] = psum.tile([P, D], F32, name="o_ps")
            nc.tensor.matmul(tiles["scale"][:], lhsT=ones_f32[:], rhs=scale_row[:], start=True, stop=True)

        def copy_scale():
            for j in range(2):
                nc.scalar.copy(out=v_scale[:, j, :], in_=tiles["scale"][:])

        issued = set()

        def once(call, m, *args):
            if 0 <= m < BLOCKS and (call, m, args) not in issued:
                issued.add((call, m, args))
                call(m, *args)

        with tc.manual_schedule():
            nc.vector.memset(scale_row[:], 0.0)
            nc.vector.memset(sk_raw[:].bitcast(I32), 0)
            nc.vector.memset(ones_f32[:], 1.0)
            nc.vector.memset(sv_raw[:].bitcast(I32), 0)
            nc.vector.memset(bc_row[:], 0.0)
            nc.vector.memset(sc[:].bitcast(I32), 0)
            nc.vector.memset(ones[:], 1.0)
            nc.scalar.dma_start(out=scale_row[0:1, :], in_=values_scale[0])
            nc.sync.dma_start(out=k_in[0][:, 0:2, :], in_=keys_m[0, :, 0:2, :])
            load_words(wk_raw, Wbk_words)
            nc.sync.dma_start(out=v_in[0][:], in_=vals_m[0])
            load_scales(sk_raw, Wbk_scales)
            nc.gpsimd.dma_start(out=k_in[0][:, 2:4, :], in_=keys_m[0, :, 2:4, :])
            nc.gpsimd.dma_start(out=bk[:], in_=bbk.rearrange("(p t) -> p t", t=PACK))
            nc.gpsimd.dma_start(out=bv[:], in_=bbv.rearrange("(p t) -> p t", t=PACK))
            nc.gpsimd.dma_start(out=bc_row[0:1, :], in_=bbc.rearrange("(o d) -> o d", o=1))
            load_words(wv_raw, Wbv_words)
            load_scales(sv_raw, Wbv_scales)
            nc.sync.dma_start(out=v_in[1][:], in_=vals_m[1])
            nc.sync.dma_start(out=k_in[1][:], in_=keys_m[1])
            load_words(wc, Wbc_words)
            load_scales(sc, Wbc_scales)
            for m in range(2, BLOCKS):
                nc.sync.dma_start(out=v_in[m][:], in_=vals_m[m])
                nc.sync.dma_start(out=k_in[m][:], in_=keys_m[m])

            spread_scale()
            permute_words(wk, wk_raw)
            permute_scales(sk, sk_raw)
            permute_words(wv, wv_raw)
            copy_scale()
            once(transpose, 0, FIRST, "k")
            once(copy_out, 0, FIRST, "k")
            once(transpose, 0, SECOND, "k")
            once(copy_out, 0, SECOND, "k")
            once(scale_values, 0, FIRST)
            once(transpose, 0, FIRST, "v")
            once(scale_values, 0, SECOND)
            permute_scales(sv, sv_raw)
            once(copy_out, 0, FIRST, "v")
            once(transpose, 0, SECOND, "v")
            once(copy_out, 0, SECOND, "v")
            once(quantize_inputs, 0, FIRST)
            once(project, 0, FIRST, "k")
            once(scale_values, 1, FIRST)
            once(project, 0, FIRST, "v")
            once(add_bias, 0, FIRST, "k")
            once(add_bias, 0, FIRST, "v")
            once(transpose, 1, FIRST, "k")
            once(transpose, 1, FIRST, "v")
            spread_bias()
            for m in range(BLOCKS + 2):
                once(quantize_product, m - 1, SECOND)
                once(copy_out, m, SECOND, "v")
                once(quantize_inputs, m, SECOND)
                once(add_bias, m, FIRST, "k")
                once(project, m, FIRST, "v")
                once(add_bias, m, FIRST, "v")
                once(copy_out, m + 1, FIRST, "k")
                once(project, m, SECOND, "k")
                once(scale_values, m + 1, SECOND)
                once(combine, m - 1, 0)
                once(bind_on_gpsimd, m)
                once(combine, m - 1, 1)
                once(project, m, SECOND, "v")
                once(add_bias, m, SECOND, "k")
                once(finish, m - 1, 0)
                once(transpose, m + 1, FIRST, "v")
                once(copy_out, m + 1, FIRST, "v")
                once(transpose, m + 1, SECOND, "k")
                once(combine, m - 1, 2)
                once(finish, m - 1, 1)
                once(combine, m - 1, 3)
                once(bind_on_vector, m, SECOND)
                once(transpose, m + 1, SECOND, "v")
                once(copy_out, m + 1, SECOND, "k")
                once(finish, m - 1, 2)
                once(finish, m - 1, 3)
                once(quantize_product, m, FIRST)
                once(quantize_inputs, m + 1, FIRST)
                once(scale_values, m + 2, FIRST)
                once(transpose, m + 2, FIRST, "k")
                once(project, m + 1, FIRST, "k")
                once(interleave, m, SECOND)
